import numpy as np
import ml_dtypes


def mxq(x, axis, fmt="e4m3"):
    dtype, down = {"e4m3": (ml_dtypes.float8_e4m3fn, 7), "e5m2": (ml_dtypes.float8_e5m2, 14)}[fmt]
    v = np.moveaxis(np.asarray(x, np.float32).astype(ml_dtypes.bfloat16).astype(np.float64), axis, -1)
    blocks = v.reshape(v.shape[:-1] + (-1, 32))
    amax = np.abs(blocks).max(-1, keepdims=True)
    byte = np.maximum(np.where(amax > 0, np.frexp(amax)[1] - 1 + 127, 0) - down, 1)
    scale = np.exp2(byte - 127.0)
    codes = (blocks / scale).astype(np.float32).astype(dtype).astype(np.float64)
    return np.moveaxis((codes * scale).reshape(v.shape), -1, axis)


WIDE = False


def mx_kscale(k):
    if not WIDE:
        return np.ones(k)
    levels = np.array([10, -10, 5, -5, 0])
    a = np.random.permutation(np.resize(levels, k // 512 * 4)).reshape(k // 512, 4)
    idx = np.arange(k)
    return np.exp2(a[idx // 512, idx % 128 // 32])


BF16 = ml_dtypes.bfloat16


def bf(x):
    return np.asarray(x, np.float32).astype(BF16)


def f64(x):
    return np.asarray(x).astype(np.float64)


E2M1 = np.array([0.0, 0.5, 1.0, 1.5, 2.0, 3.0, 4.0, 6.0, -0.0, -0.5, -1.0, -1.5, -2.0, -3.0, -4.0, -6.0])


def pack_weight(w, fmt):
    k, n = w.shape
    w = f64(bf(w)).reshape(k // 32, 32, n)
    amax = np.abs(w).max(1)
    if fmt == "e4m3":
        byte = np.frexp(amax)[1] - 1 + 127 - 7
    else:
        mant, ex = np.frexp(amax / 6.0)
        byte = np.where(mant > 0.5, ex, ex - 1) + 127
    byte = np.clip(np.where(amax > 0, byte, 1), 1, 254)
    scaled = (w * np.exp2(127.0 - byte)[:, None, :]).reshape(k, n).astype(np.float32)
    by_word = np.ascontiguousarray(scaled.reshape(k // 512, 128, 4, n).transpose(0, 1, 3, 2))
    if fmt == "e4m3":
        words = by_word.astype(ml_dtypes.float8_e4m3fn).view(np.uint8)
    else:
        c = by_word.astype(ml_dtypes.float4_e2m1fn).view(np.uint8) & 0xF
        words = c[..., 0::2] | (c[..., 1::2] << 4)
    return np.ascontiguousarray(words), np.ascontiguousarray(byte.astype(np.uint8).reshape(k // 512, 16, n))


def unpack_weight(words, scales, fmt):
    g, p, n, _ = words.shape
    if fmt == "e4m3":
        vals = np.ascontiguousarray(words).view(ml_dtypes.float8_e4m3fn).astype(np.float64)
    else:
        nib = np.empty((g, p, n, 4), np.uint8)
        nib[..., 0::2] = words & 0xF
        nib[..., 1::2] = words >> 4
        vals = E2M1[nib]
    vals = vals * np.repeat(np.exp2(scales.astype(np.float64) - 127.0), 8, axis=1)[..., None]
    return vals.transpose(0, 1, 3, 2).reshape(g * 512, n)

def pack4(w):
    words, scales = pack_weight(w, "e2m1")
    return words.reshape(words.shape[0], 128, -1), scales


def unpack4(words, scales):
    return unpack_weight(words.reshape(words.shape[0], 128, -1, 2), scales, "e2m1")


B, S, E, H = 2, 256, 512, 4
D = E // H
LN_EPS = 1e-6


def setup_inputs():
    s = mx_kscale(E)
    h_attn = bf(np.random.standard_normal((B, H, S, D)) * 0.4 * s.reshape(H, 1, D))
    x = bf(np.random.standard_normal((B, S, E)))
    out_w_words, out_w_scales = pack4(np.random.standard_normal((E, E)) * 2.0 / np.sqrt(E) / s[:, None])
    ln_gamma = bf(1.0 + 0.1 * np.random.standard_normal(E))
    ln_beta = bf(0.1 * np.random.standard_normal(E))
    return {"h_attn": h_attn,
            "x": x,
            "out_w_words": out_w_words,
            "out_w_scales": out_w_scales,
            "ln_gamma": ln_gamma,
            "ln_beta": ln_beta}


def reference(h_attn, x, out_w_words, out_w_scales, ln_gamma, ln_beta):
    merged = f64(h_attn).transpose(0, 2, 1, 3).reshape(B, S, E)
    out = mxq(merged, 2, "e4m3") @ unpack4(out_w_words, out_w_scales)
    y = out + f64(x)
    mean = y.mean(-1, keepdims=True)
    var = np.square(y - mean).mean(-1, keepdims=True)
    return (y - mean) / np.sqrt(var + LN_EPS) * f64(ln_gamma) + f64(ln_beta)

@@ -1,0 +1,125 @@
+from contextlib import ExitStack
+
+import concourse.mybir as mybir
+from concourse.masks import make_identity
+
+F32 = mybir.dt.float32
+BF16 = mybir.dt.bfloat16
+I32 = mybir.dt.int32
+U32 = mybir.dt.uint32
+U8 = mybir.dt.uint8
+FP8X4 = mybir.dt.float8_e4m3fn_x4
+FP4X4 = mybir.dt.float4_e2m1fn_x4
+ALU = mybir.AluOpType
+ACT = mybir.ActivationFunctionType
+
+P = 128
+B, H, S, D = 2, 4, 256, 128
+E = H * D
+S_BLOCKS = S // P
+TILES = B * S_BLOCKS
+WORDS = E // 2
+LN_EPS = 1e-6
+
+FLOPS = 2 * B * S * E * E
+
+
+def tile_selfattention_pa_s_kernel(tc, h_attn, x, out_w_words, out_w_scales, ln_gamma, ln_beta, out):
+    nc = tc.nc
+    with ExitStack() as ctx:
+        keep = ctx.enter_context(tc.tile_pool(name="keep", bufs=1))
+        work = ctx.enter_context(tc.tile_pool(name="work", bufs=TILES))
+        psum_t = ctx.enter_context(tc.psum_pool(name="psum_t", bufs=2))
+        psum_acc = ctx.enter_context(tc.psum_pool(name="psum_acc", bufs=TILES))
+
+        h_sb = keep.tile([P, TILES, E], BF16)
+        x_sb = keep.tile([P, TILES, E], BF16)
+        w_words = keep.tile([P, 2 * E], U8, align_bytes=64)
+        w_plane = keep.tile([P, E], U8, align_bytes=64)
+        gamma_b = keep.tile([P, E], BF16)
+        beta_b = keep.tile([P, E], BF16)
+
+        def load_h(j):
+            positions = slice(j * P, (j + 1) * P)
+            nc.sync.dma_start(
+                out=h_sb[:, B * j : B * (j + 1), :].rearrange("p t (h d) -> p (t h) d", d=D),
+                in_=h_attn[:, :, positions, :].rearrange("b h s d -> s (b h) d"),
+            )
+
+        def load_x(j):
+            positions = slice(j * P, (j + 1) * P)
+            nc.sync.dma_start(
+                out=x_sb[:, B * j : B * (j + 1), :],
+                in_=x[:, positions, :].rearrange("b s e -> s b e"),
+            )
+
+        nc.vector.memset(w_plane[:].bitcast(I32), 0)
+        load_h(0)
+        nc.sync.dma_start(out=w_words[:].bitcast(I32), in_=out_w_words[0].bitcast(I32))
+        for r in range(4):
+            nc.sync.dma_start(out=w_plane[r:P:32, :].bitcast(I32), in_=out_w_scales[0, r:16:4, :].bitcast(I32))
+        load_x(0)
+        load_h(1)
+        load_x(1)
+        nc.scalar.dma_start(out=gamma_b[:], in_=ln_gamma.partition_broadcast(P))
+        nc.scalar.dma_start(out=beta_b[:], in_=ln_beta.partition_broadcast(P))
+
+        ident = keep.tile([P, P], F32)
+        make_identity(nc, ident[:])
+
+        one = keep.tile([P, 1], F32)
+        warm = keep.tile([P, 1], F32)
+        nc.vector.memset(one[:], 1.0)
+        nc.scalar.sqrt(warm[:], one[:])
+
+        accs = []
+        for t in range(TILES):
+            h_words = h_sb[:, t, :].bitcast(F32)
+            planes = psum_t.tile([P, 2, P], F32)
+            for u in range(2):
+                nc.tensor.transpose(planes[:, u, :], h_words[:, u:WORDS:2], ident[:])
+            grouped = work.tile([P, 4 * P], BF16, align_bytes=64)
+            nc.scalar.copy(
+                out=grouped[:].bitcast(F32).rearrange("p (r u) -> p r u", u=2),
+                in_=planes[:].rearrange("p u r -> p r u"),
+            )
+            m_codes = work.tile([P, P], U32, align_bytes=64)
+            m_scales = work.tile([P, P], U8, align_bytes=64)
+            nc.vector.quantize_mx(out=m_codes[:].bitcast(FP8X4), scales=m_scales[:], in_=grouped[:])
+            acc = psum_acc.tile([P, E], F32)
+            nc.tensor.matmul_mx(
+                out=acc[:],
+                lhsT=m_codes[:].bitcast(FP8X4),
+                lhsT_scale=m_scales[:],
+                rhs=w_words[:].bitcast(FP4X4),
+                rhs_scale=w_plane[:],
+                start=True,
+                stop=True,
+            )
+            accs.append(acc)
+
+        for t in range(TILES):
+            j, b = divmod(t, B)
+            y = work.tile([P, E], F32)
+            y_sum = work.tile([P, 1], F32)
+            nc.vector.scalar_tensor_tensor(
+                out=y[:], in0=accs[t][:], scalar=1.0, in1=x_sb[:, t, :], op0=ALU.mult, op1=ALU.add, accum_out=y_sum[:]
+            )
+            neg_mean = work.tile([P, 1], F32)
+            nc.scalar.mul(neg_mean[:], y_sum[:], -1.0 / E)
+            squares = work.tile([P, E], F32)
+            sq_sum = work.tile([P, 1], F32)
+            nc.scalar.activation(out=squares[:], in_=y[:], func=ACT.Square, bias=neg_mean[:], scale=1.0, accum_out=sq_sum[:])
+            std = work.tile([P, 1], F32)
+            nc.scalar.activation(out=std[:], in_=sq_sum[:], func=ACT.Sqrt, bias=LN_EPS, scale=1.0 / E)
+            rstd = work.tile([P, 1], F32)
+            nc.vector.reciprocal(rstd[:], std[:])
+            centred = work.tile([P, E], F32)
+            nc.vector.scalar_tensor_tensor(
+                out=centred[:], in0=y[:], scalar=neg_mean[:], in1=gamma_b[:], op0=ALU.add, op1=ALU.mult
+            )
+            result = work.tile([P, E], F32)
+            nc.vector.scalar_tensor_tensor(
+                out=result[:], in0=centred[:], scalar=rstd[:], in1=beta_b[:], op0=ALU.mult, op1=ALU.add
+            )
+            nc.sync.dma_start(out=out[b, j * P : (j + 1) * P, :], in_=result[:])

@@ -19,6 +19,7 @@ E = H * D
 S_BLOCKS = S // P
 TILES = B * S_BLOCKS
 WORDS = E // 2
+E_CHUNKS = E // P
 LN_EPS = 1e-6
 
 FLOPS = 2 * B * S * E * E
@@ -27,99 +28,138 @@ FLOPS = 2 * B * S * E * E
 def tile_selfattention_pa_s_kernel(tc, h_attn, x, out_w_words, out_w_scales, ln_gamma, ln_beta, out):
     nc = tc.nc
     with ExitStack() as ctx:
+        ctx.enter_context(tc.manual_schedule())
         keep = ctx.enter_context(tc.tile_pool(name="keep", bufs=1))
+        pairs = ctx.enter_context(tc.tile_pool(name="pairs", bufs=S_BLOCKS))
         work = ctx.enter_context(tc.tile_pool(name="work", bufs=TILES))
-        psum_t = ctx.enter_context(tc.psum_pool(name="psum_t", bufs=2))
         psum_acc = ctx.enter_context(tc.psum_pool(name="psum_acc", bufs=TILES))
+        psum_t = ctx.enter_context(tc.psum_pool(name="psum_t", bufs=S_BLOCKS))
+        psum_gb = ctx.enter_context(tc.psum_pool(name="psum_gb", bufs=1))
 
         h_sb = keep.tile([P, TILES, E], BF16)
         x_sb = keep.tile([P, TILES, E], BF16)
         w_words = keep.tile([P, 2 * E], U8, align_bytes=64)
         w_plane = keep.tile([P, E], U8, align_bytes=64)
-        gamma_b = keep.tile([P, E], BF16)
-        beta_b = keep.tile([P, E], BF16)
+        gb_rows = keep.tile([P, P], BF16)
 
-        def load_h(j):
-            positions = slice(j * P, (j + 1) * P)
+        nc.vector.memset(gb_rows[:].bitcast(I32), 0)
+        nc.vector.memset(w_plane[:].bitcast(I32), 0)
+        nc.scalar.dma_start(out=gb_rows[0:E_CHUNKS, :], in_=ln_gamma.rearrange("(c k) -> c k", k=P))
+        nc.scalar.dma_start(out=gb_rows[E_CHUNKS : 2 * E_CHUNKS, :], in_=ln_beta.rearrange("(c k) -> c k", k=P))
+        for j in range(S_BLOCKS):
             nc.sync.dma_start(
                 out=h_sb[:, B * j : B * (j + 1), :].rearrange("p t (h d) -> p (t h) d", d=D),
-                in_=h_attn[:, :, positions, :].rearrange("b h s d -> s (b h) d"),
+                in_=h_attn[:, :, j * P : (j + 1) * P, :].rearrange("b h s d -> s (b h) d"),
             )
-
-        def load_x(j):
-            positions = slice(j * P, (j + 1) * P)
-            nc.sync.dma_start(
-                out=x_sb[:, B * j : B * (j + 1), :],
-                in_=x[:, positions, :].rearrange("b s e -> s b e"),
-            )
-
-        nc.vector.memset(w_plane[:].bitcast(I32), 0)
-        load_h(0)
         nc.sync.dma_start(out=w_words[:].bitcast(I32), in_=out_w_words[0].bitcast(I32))
         for r in range(4):
             nc.sync.dma_start(out=w_plane[r:P:32, :].bitcast(I32), in_=out_w_scales[0, r:16:4, :].bitcast(I32))
-        load_x(0)
-        load_h(1)
-        load_x(1)
-        nc.scalar.dma_start(out=gamma_b[:], in_=ln_gamma.partition_broadcast(P))
-        nc.scalar.dma_start(out=beta_b[:], in_=ln_beta.partition_broadcast(P))
+        for j in range(S_BLOCKS):
+            nc.sync.dma_start(
+                out=x_sb[:, B * j : B * (j + 1), :],
+                in_=x[:, j * P : (j + 1) * P, :].rearrange("b s e -> s b e"),
+            )
 
         ident = keep.tile([P, P], F32)
+        ident_bf = keep.tile([P, P], BF16)
         make_identity(nc, ident[:])
+        nc.vector.tensor_copy(out=ident_bf[:], in_=ident[:])
 
         one = keep.tile([P, 1], F32)
         warm = keep.tile([P, 1], F32)
         nc.vector.memset(one[:], 1.0)
         nc.scalar.sqrt(warm[:], one[:])
 
-        accs = []
-        for t in range(TILES):
-            h_words = h_sb[:, t, :].bitcast(F32)
-            planes = psum_t.tile([P, 2, P], F32)
-            for u in range(2):
-                nc.tensor.transpose(planes[:, u, :], h_words[:, u:WORDS:2], ident[:])
-            grouped = work.tile([P, 4 * P], BF16, align_bytes=64)
-            nc.scalar.copy(
-                out=grouped[:].bitcast(F32).rearrange("p (r u) -> p r u", u=2),
-                in_=planes[:].rearrange("p u r -> p r u"),
-            )
-            m_codes = work.tile([P, P], U32, align_bytes=64)
-            m_scales = work.tile([P, P], U8, align_bytes=64)
-            nc.vector.quantize_mx(out=m_codes[:].bitcast(FP8X4), scales=m_scales[:], in_=grouped[:])
-            acc = psum_acc.tile([P, E], F32)
-            nc.tensor.matmul_mx(
-                out=acc[:],
-                lhsT=m_codes[:].bitcast(FP8X4),
-                lhsT_scale=m_scales[:],
-                rhs=w_words[:].bitcast(FP4X4),
-                rhs_scale=w_plane[:],
-                start=True,
-                stop=True,
-            )
-            accs.append(acc)
+        gb_t = psum_gb.tile([P, P], BF16)
+        nc.tensor.transpose(gb_t[:], gb_rows[:], ident_bf[:])
+        gb_cols = keep.tile([P, 2 * E_CHUNKS], BF16)
+        nc.scalar.copy(out=gb_cols[:], in_=gb_t[:, 0 : 2 * E_CHUNKS])
 
-        for t in range(TILES):
-            j, b = divmod(t, B)
-            y = work.tile([P, E], F32)
-            y_sum = work.tile([P, 1], F32)
-            nc.vector.scalar_tensor_tensor(
-                out=y[:], in0=accs[t][:], scalar=1.0, in1=x_sb[:, t, :], op0=ALU.mult, op1=ALU.add, accum_out=y_sum[:]
+        def transpose_pair(j):
+            planes = psum_t.tile([P, B, 2, P], F32)
+            for b in range(B):
+                h_words = h_sb[:, B * j + b, :].bitcast(F32)
+                for u in range(2):
+                    nc.tensor.transpose(planes[:, b, u, :], h_words[:, u:WORDS:2], ident[:])
+            return planes
+
+        planes_of = [transpose_pair(0)]
+        gb_all = psum_gb.tile([P, 2 * E_CHUNKS, P], BF16)
+        for r in range(2 * E_CHUNKS):
+            nc.tensor.transpose(gb_all[:, r, :], gb_cols[:, r : r + 1].to_broadcast([P, P]), ident_bf[:])
+        gamma_all = gb_all[:, 0:E_CHUNKS, :].rearrange("p c k -> p (c k)")
+        beta_all = gb_all[:, E_CHUNKS : 2 * E_CHUNKS, :].rearrange("p c k -> p (c k)")
+        planes_of.append(transpose_pair(1))
+
+        accs = []
+        for j in range(S_BLOCKS):
+            grouped = pairs.tile([P, B, 4 * P], BF16, align_bytes=64)
+            nc.scalar.copy(
+                out=grouped[:].bitcast(F32).rearrange("p b (r u) -> p b r u", u=2),
+                in_=planes_of[j][:].rearrange("p b u r -> p b r u"),
             )
-            neg_mean = work.tile([P, 1], F32)
-            nc.scalar.mul(neg_mean[:], y_sum[:], -1.0 / E)
+            m_codes = pairs.tile([P, B, P], U32, align_bytes=64)
+            m_scales = pairs.tile([P, B, P], U8, align_bytes=64)
+            nc.vector.quantize_mx(
+                out=m_codes[:].rearrange("p b r -> p (b r)").bitcast(FP8X4),
+                scales=m_scales[:].rearrange("p b r -> p (b r)"),
+                in_=grouped[:].rearrange("p b c -> p (b c)"),
+            )
+            for b in range(B):
+                acc = psum_acc.tile([P, E], F32)
+                nc.tensor.matmul_mx(
+                    out=acc[:],
+                    lhsT=m_codes[:, b, :].bitcast(FP8X4),
+                    lhsT_scale=m_scales[:, b, :],
+                    rhs=w_words[:].bitcast(FP4X4),
+                    rhs_scale=w_plane[:],
+                    start=True,
+                    stop=True,
+                )
+                accs.append(acc)
+
+        y_sum = keep.tile([P, TILES], F32)
+        neg_mean = keep.tile([P, TILES], F32)
+        sq_sum = keep.tile([P, TILES], F32)
+        std = keep.tile([P, TILES], F32)
+        rstd = keep.tile([P, TILES], F32)
+        ys = []
+        for t in range(TILES):
+            y = work.tile([P, E], F32)
+            nc.vector.scalar_tensor_tensor(
+                out=y[:],
+                in0=accs[t][:],
+                scalar=1.0,
+                in1=x_sb[:, t, :],
+                op0=ALU.mult,
+                op1=ALU.add,
+                accum_out=y_sum[:, t : t + 1],
+            )
+            nc.scalar.mul(neg_mean[:, t : t + 1], y_sum[:, t : t + 1], -1.0 / E)
             squares = work.tile([P, E], F32)
-            sq_sum = work.tile([P, 1], F32)
-            nc.scalar.activation(out=squares[:], in_=y[:], func=ACT.Square, bias=neg_mean[:], scale=1.0, accum_out=sq_sum[:])
-            std = work.tile([P, 1], F32)
-            nc.scalar.activation(out=std[:], in_=sq_sum[:], func=ACT.Sqrt, bias=LN_EPS, scale=1.0 / E)
-            rstd = work.tile([P, 1], F32)
-            nc.vector.reciprocal(rstd[:], std[:])
+            nc.scalar.activation(
+                out=squares[:],
+                in_=y[:],
+                func=ACT.Square,
+                bias=neg_mean[:, t : t + 1],
+                scale=1.0,
+                accum_out=sq_sum[:, t : t + 1],
+            )
+            ys.append(y)
+        nc.scalar.activation(out=std[:], in_=sq_sum[:], func=ACT.Sqrt, bias=LN_EPS, scale=1.0 / E)
+
+        centred_of = []
+        for t in range(TILES):
             centred = work.tile([P, E], F32)
             nc.vector.scalar_tensor_tensor(
-                out=centred[:], in0=y[:], scalar=neg_mean[:], in1=gamma_b[:], op0=ALU.add, op1=ALU.mult
+                out=centred[:], in0=ys[t][:], scalar=neg_mean[:, t : t + 1], in1=gamma_all, op0=ALU.add, op1=ALU.mult
             )
+            centred_of.append(centred)
+        nc.vector.reciprocal(rstd[:], std[:])
+        for t in range(TILES):
+            j, b = divmod(t, B)
             result = work.tile([P, E], F32)
             nc.vector.scalar_tensor_tensor(
-                out=result[:], in0=centred[:], scalar=rstd[:], in1=beta_b[:], op0=ALU.mult, op1=ALU.add
+                out=result[:], in0=centred_of[t][:], scalar=rstd[:, t : t + 1], in1=beta_all, op0=ALU.mult, op1=ALU.add
             )
             nc.sync.dma_start(out=out[b, j * P : (j + 1) * P, :], in_=result[:])

@@ -30,10 +30,8 @@ def tile_selfattention_pa_s_kernel(tc, h_attn, x, out_w_words, out_w_scales, ln_
     with ExitStack() as ctx:
         ctx.enter_context(tc.manual_schedule())
         keep = ctx.enter_context(tc.tile_pool(name="keep", bufs=1))
-        pairs = ctx.enter_context(tc.tile_pool(name="pairs", bufs=S_BLOCKS))
         work = ctx.enter_context(tc.tile_pool(name="work", bufs=TILES))
-        psum_acc = ctx.enter_context(tc.psum_pool(name="psum_acc", bufs=TILES))
-        psum_t = ctx.enter_context(tc.psum_pool(name="psum_t", bufs=S_BLOCKS))
+        psum = ctx.enter_context(tc.psum_pool(name="psum", bufs=TILES))
         psum_gb = ctx.enter_context(tc.psum_pool(name="psum_gb", bufs=1))
 
         h_sb = keep.tile([P, TILES, E], BF16)
@@ -41,11 +39,12 @@ def tile_selfattention_pa_s_kernel(tc, h_attn, x, out_w_words, out_w_scales, ln_
         w_words = keep.tile([P, 2 * E], U8, align_bytes=64)
         w_plane = keep.tile([P, E], U8, align_bytes=64)
         gb_rows = keep.tile([P, P], BF16)
+        ident = keep.tile([P, P], F32)
+        ident_bf = keep.tile([P, P], BF16)
+        one = keep.tile([P, 1], F32)
+        warm = keep.tile([P, 1], F32)
 
-        nc.vector.memset(gb_rows[:].bitcast(I32), 0)
         nc.vector.memset(w_plane[:].bitcast(I32), 0)
-        nc.scalar.dma_start(out=gb_rows[0:E_CHUNKS, :], in_=ln_gamma.rearrange("(c k) -> c k", k=P))
-        nc.scalar.dma_start(out=gb_rows[E_CHUNKS : 2 * E_CHUNKS, :], in_=ln_beta.rearrange("(c k) -> c k", k=P))
         for j in range(S_BLOCKS):
             nc.sync.dma_start(
                 out=h_sb[:, B * j : B * (j + 1), :].rearrange("p t (h d) -> p (t h) d", d=D),
@@ -59,64 +58,50 @@ def tile_selfattention_pa_s_kernel(tc, h_attn, x, out_w_words, out_w_scales, ln_
                 out=x_sb[:, B * j : B * (j + 1), :],
                 in_=x[:, j * P : (j + 1) * P, :].rearrange("b s e -> s b e"),
             )
-
-        ident = keep.tile([P, P], F32)
-        ident_bf = keep.tile([P, P], BF16)
+        nc.gpsimd.memset(gb_rows[:], 0.0)
+        nc.gpsimd.dma_start(out=gb_rows[0:E_CHUNKS, :], in_=ln_gamma.rearrange("(c k) -> c k", k=P))
+        nc.gpsimd.dma_start(out=gb_rows[E_CHUNKS : 2 * E_CHUNKS, :], in_=ln_beta.rearrange("(c k) -> c k", k=P))
         make_identity(nc, ident[:])
-        nc.vector.tensor_copy(out=ident_bf[:], in_=ident[:])
-
-        one = keep.tile([P, 1], F32)
-        warm = keep.tile([P, 1], F32)
         nc.vector.memset(one[:], 1.0)
+        nc.vector.tensor_copy(out=ident_bf[:], in_=ident[:])
         nc.scalar.sqrt(warm[:], one[:])
 
+        banks = []
+        for t in range(TILES):
+            bank = psum.tile([P, E], F32)
+            h_words = h_sb[:, t, :].bitcast(F32)
+            for u in range(2):
+                nc.tensor.transpose(bank[:, u * P : (u + 1) * P], h_words[:, u:WORDS:2], ident[:])
+            banks.append(bank)
         gb_t = psum_gb.tile([P, P], BF16)
         nc.tensor.transpose(gb_t[:], gb_rows[:], ident_bf[:])
+
+        for t in range(TILES):
+            grouped = work.tile([P, 4 * P], BF16, align_bytes=64)
+            nc.scalar.copy(
+                out=grouped[:].bitcast(F32).rearrange("p (r u) -> p r u", u=2),
+                in_=banks[t][:, 0 : 2 * P].rearrange("p (u r) -> p r u", u=2),
+            )
+            m_codes = work.tile([P, P], U32, align_bytes=64)
+            m_scales = work.tile([P, P], U8, align_bytes=64)
+            nc.vector.quantize_mx(out=m_codes[:].bitcast(FP8X4), scales=m_scales[:], in_=grouped[:])
+            nc.tensor.matmul_mx(
+                out=banks[t][:],
+                lhsT=m_codes[:].bitcast(FP8X4),
+                lhsT_scale=m_scales[:],
+                rhs=w_words[:].bitcast(FP4X4),
+                rhs_scale=w_plane[:],
+                start=True,
+                stop=True,
+            )
+
         gb_cols = keep.tile([P, 2 * E_CHUNKS], BF16)
         nc.scalar.copy(out=gb_cols[:], in_=gb_t[:, 0 : 2 * E_CHUNKS])
-
-        def transpose_pair(j):
-            planes = psum_t.tile([P, B, 2, P], F32)
-            for b in range(B):
-                h_words = h_sb[:, B * j + b, :].bitcast(F32)
-                for u in range(2):
-                    nc.tensor.transpose(planes[:, b, u, :], h_words[:, u:WORDS:2], ident[:])
-            return planes
-
-        planes_of = [transpose_pair(0)]
         gb_all = psum_gb.tile([P, 2 * E_CHUNKS, P], BF16)
         for r in range(2 * E_CHUNKS):
             nc.tensor.transpose(gb_all[:, r, :], gb_cols[:, r : r + 1].to_broadcast([P, P]), ident_bf[:])
         gamma_all = gb_all[:, 0:E_CHUNKS, :].rearrange("p c k -> p (c k)")
         beta_all = gb_all[:, E_CHUNKS : 2 * E_CHUNKS, :].rearrange("p c k -> p (c k)")
-        planes_of.append(transpose_pair(1))
-
-        accs = []
-        for j in range(S_BLOCKS):
-            grouped = pairs.tile([P, B, 4 * P], BF16, align_bytes=64)
-            nc.scalar.copy(
-                out=grouped[:].bitcast(F32).rearrange("p b (r u) -> p b r u", u=2),
-                in_=planes_of[j][:].rearrange("p b u r -> p b r u"),
-            )
-            m_codes = pairs.tile([P, B, P], U32, align_bytes=64)
-            m_scales = pairs.tile([P, B, P], U8, align_bytes=64)
-            nc.vector.quantize_mx(
-                out=m_codes[:].rearrange("p b r -> p (b r)").bitcast(FP8X4),
-                scales=m_scales[:].rearrange("p b r -> p (b r)"),
-                in_=grouped[:].rearrange("p b c -> p (b c)"),
-            )
-            for b in range(B):
-                acc = psum_acc.tile([P, E], F32)
-                nc.tensor.matmul_mx(
-                    out=acc[:],
-                    lhsT=m_codes[:, b, :].bitcast(FP8X4),
-                    lhsT_scale=m_scales[:, b, :],
-                    rhs=w_words[:].bitcast(FP4X4),
-                    rhs_scale=w_plane[:],
-                    start=True,
-                    stop=True,
-                )
-                accs.append(acc)
 
         y_sum = keep.tile([P, TILES], F32)
         neg_mean = keep.tile([P, TILES], F32)
@@ -128,14 +113,21 @@ def tile_selfattention_pa_s_kernel(tc, h_attn, x, out_w_words, out_w_scales, ln_
             y = work.tile([P, E], F32)
             nc.vector.scalar_tensor_tensor(
                 out=y[:],
-                in0=accs[t][:],
+                in0=banks[t][:],
                 scalar=1.0,
                 in1=x_sb[:, t, :],
                 op0=ALU.mult,
                 op1=ALU.add,
                 accum_out=y_sum[:, t : t + 1],
             )
-            nc.scalar.mul(neg_mean[:, t : t + 1], y_sum[:, t : t + 1], -1.0 / E)
+            nc.gpsimd.tensor_scalar(
+                out=neg_mean[:, t : t + 1],
+                in0=y_sum[:, t : t + 1],
+                scalar1=-1.0 / E,
+                scalar2=0.0,
+                op0=ALU.mult,
+                op1=ALU.add,
+            )
             squares = work.tile([P, E], F32)
             nc.scalar.activation(
                 out=squares[:],

@@ -21,6 +21,7 @@ TILES = B * S_BLOCKS
 WORDS = E // 2
 E_CHUNKS = E // P
 LN_EPS = 1e-6
+SHARED_TILE = TILES - 2
 
 FLOPS = 2 * B * S * E * E
 
@@ -58,6 +59,8 @@ def tile_selfattention_pa_s_kernel(tc, h_attn, x, out_w_words, out_w_scales, ln_
                 out=x_sb[:, B * j : B * (j + 1), :],
                 in_=x[:, j * P : (j + 1) * P, :].rearrange("b s e -> s b e"),
             )
+        beta_sb = keep.tile([P, E], BF16)
+        nc.sync.dma_start(out=beta_sb[:], in_=ln_beta.partition_broadcast(P))
         nc.gpsimd.memset(gb_rows[:], 0.0)
         nc.gpsimd.dma_start(out=gb_rows[0:E_CHUNKS, :], in_=ln_gamma.rearrange("(c k) -> c k", k=P))
         nc.gpsimd.dma_start(out=gb_rows[E_CHUNKS : 2 * E_CHUNKS, :], in_=ln_beta.rearrange("(c k) -> c k", k=P))
@@ -151,7 +154,17 @@ def tile_selfattention_pa_s_kernel(tc, h_attn, x, out_w_words, out_w_scales, ln_
         for t in range(TILES):
             j, b = divmod(t, B)
             result = work.tile([P, E], F32)
-            nc.vector.scalar_tensor_tensor(
-                out=result[:], in0=centred_of[t][:], scalar=rstd[:, t : t + 1], in1=beta_all, op0=ALU.mult, op1=ALU.add
-            )
+            if t == SHARED_TILE:
+                scaled = keep.tile([P, E], F32)
+                nc.scalar.activation(out=scaled[:], in_=centred_of[t][:], func=ACT.Copy, scale=rstd[:, t : t + 1])
+                nc.gpsimd.tensor_tensor(out=result[:], in0=scaled[:], in1=beta_sb[:], op=ALU.add)
+            else:
+                nc.vector.scalar_tensor_tensor(
+                    out=result[:],
+                    in0=centred_of[t][:],
+                    scalar=rstd[:, t : t + 1],
+                    in1=beta_all,
+                    op0=ALU.mult,
+                    op1=ALU.add,
+                )
             nc.sync.dma_start(out=out[b, j * P : (j + 1) * P, :], in_=result[:])

@@ -21,7 +21,6 @@ TILES = B * S_BLOCKS
 WORDS = E // 2
 E_CHUNKS = E // P
 LN_EPS = 1e-6
-SHARED_TILE = TILES - 2
 
 FLOPS = 2 * B * S * E * E
 
@@ -59,15 +58,13 @@ def tile_selfattention_pa_s_kernel(tc, h_attn, x, out_w_words, out_w_scales, ln_
                 out=x_sb[:, B * j : B * (j + 1), :],
                 in_=x[:, j * P : (j + 1) * P, :].rearrange("b s e -> s b e"),
             )
-        beta_sb = keep.tile([P, E], BF16)
-        nc.sync.dma_start(out=beta_sb[:], in_=ln_beta.partition_broadcast(P))
+        make_identity(nc, ident[:])
         nc.gpsimd.memset(gb_rows[:], 0.0)
         nc.gpsimd.dma_start(out=gb_rows[0:E_CHUNKS, :], in_=ln_gamma.rearrange("(c k) -> c k", k=P))
         nc.gpsimd.dma_start(out=gb_rows[E_CHUNKS : 2 * E_CHUNKS, :], in_=ln_beta.rearrange("(c k) -> c k", k=P))
-        make_identity(nc, ident[:])
         nc.vector.memset(one[:], 1.0)
         nc.vector.tensor_copy(out=ident_bf[:], in_=ident[:])
-        nc.scalar.sqrt(warm[:], one[:])
+        nc.scalar.activation(out=warm[:], in_=one[:], func=ACT.Abs_reciprocal_sqrt)
 
         banks = []
         for t in range(TILES):
@@ -76,10 +73,8 @@ def tile_selfattention_pa_s_kernel(tc, h_attn, x, out_w_words, out_w_scales, ln_
             for u in range(2):
                 nc.tensor.transpose(bank[:, u * P : (u + 1) * P], h_words[:, u:WORDS:2], ident[:])
             banks.append(bank)
-        gb_t = psum_gb.tile([P, P], BF16)
-        nc.tensor.transpose(gb_t[:], gb_rows[:], ident_bf[:])
 
-        for t in range(TILES):
+        def quantise_and_multiply(t):
             grouped = work.tile([P, 4 * P], BF16, align_bytes=64)
             nc.scalar.copy(
                 out=grouped[:].bitcast(F32).rearrange("p (r u) -> p r u", u=2),
@@ -98,18 +93,31 @@ def tile_selfattention_pa_s_kernel(tc, h_attn, x, out_w_words, out_w_scales, ln_
                 stop=True,
             )
 
+        gb_t = psum_gb.tile([P, P], BF16)
+        for t in range(TILES // 2):
+            quantise_and_multiply(t)
+        nc.tensor.transpose(gb_t[:], gb_rows[:], ident_bf[:])
+        for t in range(TILES // 2, TILES):
+            quantise_and_multiply(t)
+
         gb_cols = keep.tile([P, 2 * E_CHUNKS], BF16)
         nc.scalar.copy(out=gb_cols[:], in_=gb_t[:, 0 : 2 * E_CHUNKS])
-        gb_all = psum_gb.tile([P, 2 * E_CHUNKS, P], BF16)
-        for r in range(2 * E_CHUNKS):
-            nc.tensor.transpose(gb_all[:, r, :], gb_cols[:, r : r + 1].to_broadcast([P, P]), ident_bf[:])
-        gamma_all = gb_all[:, 0:E_CHUNKS, :].rearrange("p c k -> p (c k)")
-        beta_all = gb_all[:, E_CHUNKS : 2 * E_CHUNKS, :].rearrange("p c k -> p (c k)")
+        gamma_all = psum_gb.tile([P, E], BF16)
+        beta_all = psum_gb.tile([P, E], BF16)
+        for c in range(E_CHUNKS):
+            nc.tensor.transpose(
+                gamma_all[:, c * P : (c + 1) * P], gb_cols[:, c : c + 1].to_broadcast([P, P]), ident_bf[:]
+            )
+        for c in range(E_CHUNKS):
+            nc.tensor.transpose(
+                beta_all[:, c * P : (c + 1) * P],
+                gb_cols[:, E_CHUNKS + c : E_CHUNKS + c + 1].to_broadcast([P, P]),
+                ident_bf[:],
+            )
 
         y_sum = keep.tile([P, TILES], F32)
         neg_mean = keep.tile([P, TILES], F32)
         sq_sum = keep.tile([P, TILES], F32)
-        std = keep.tile([P, TILES], F32)
         rstd = keep.tile([P, TILES], F32)
         ys = []
         for t in range(TILES):
@@ -141,30 +149,19 @@ def tile_selfattention_pa_s_kernel(tc, h_attn, x, out_w_words, out_w_scales, ln_
                 accum_out=sq_sum[:, t : t + 1],
             )
             ys.append(y)
-        nc.scalar.activation(out=std[:], in_=sq_sum[:], func=ACT.Sqrt, bias=LN_EPS, scale=1.0 / E)
+        nc.scalar.activation(out=rstd[:], in_=sq_sum[:], func=ACT.Abs_reciprocal_sqrt, bias=LN_EPS, scale=1.0 / E)
 
         centred_of = []
         for t in range(TILES):
             centred = work.tile([P, E], F32)
             nc.vector.scalar_tensor_tensor(
-                out=centred[:], in0=ys[t][:], scalar=neg_mean[:, t : t + 1], in1=gamma_all, op0=ALU.add, op1=ALU.mult
+                out=centred[:], in0=ys[t][:], scalar=neg_mean[:, t : t + 1], in1=gamma_all[:], op0=ALU.add, op1=ALU.mult
             )
             centred_of.append(centred)
-        nc.vector.reciprocal(rstd[:], std[:])
         for t in range(TILES):
             j, b = divmod(t, B)
             result = work.tile([P, E], F32)
-            if t == SHARED_TILE:
-                scaled = keep.tile([P, E], F32)
-                nc.scalar.activation(out=scaled[:], in_=centred_of[t][:], func=ACT.Copy, scale=rstd[:, t : t + 1])
-                nc.gpsimd.tensor_tensor(out=result[:], in0=scaled[:], in1=beta_sb[:], op=ALU.add)
-            else:
-                nc.vector.scalar_tensor_tensor(
-                    out=result[:],
-                    in0=centred_of[t][:],
-                    scalar=rstd[:, t : t + 1],
-                    in1=beta_all,
-                    op0=ALU.mult,
-                    op1=ALU.add,
-                )
+            nc.vector.scalar_tensor_tensor(
+                out=result[:], in0=centred_of[t][:], scalar=rstd[:, t : t + 1], in1=beta_all[:], op0=ALU.mult, op1=ALU.add
+            )
             nc.sync.dma_start(out=out[b, j * P : (j + 1) * P, :], in_=result[:])

@@ -21,6 +21,7 @@ TILES = B * S_BLOCKS
 WORDS = E // 2
 E_CHUNKS = E // P
 LN_EPS = 1e-6
+GPSIMD_TILE = TILES - 1
 
 FLOPS = 2 * B * S * E * E
 
@@ -58,6 +59,8 @@ def tile_selfattention_pa_s_kernel(tc, h_attn, x, out_w_words, out_w_scales, ln_
                 out=x_sb[:, B * j : B * (j + 1), :],
                 in_=x[:, j * P : (j + 1) * P, :].rearrange("b s e -> s b e"),
             )
+        gamma_sb = keep.tile([P, E], BF16)
+        nc.sync.dma_start(out=gamma_sb[:], in_=ln_gamma.partition_broadcast(P))
         make_identity(nc, ident[:])
         nc.gpsimd.memset(gb_rows[:], 0.0)
         nc.gpsimd.dma_start(out=gb_rows[0:E_CHUNKS, :], in_=ln_gamma.rearrange("(c k) -> c k", k=P))
@@ -154,9 +157,21 @@ def tile_selfattention_pa_s_kernel(tc, h_attn, x, out_w_words, out_w_scales, ln_
         centred_of = []
         for t in range(TILES):
             centred = work.tile([P, E], F32)
-            nc.vector.scalar_tensor_tensor(
-                out=centred[:], in0=ys[t][:], scalar=neg_mean[:, t : t + 1], in1=gamma_all[:], op0=ALU.add, op1=ALU.mult
-            )
+            if t == GPSIMD_TILE:
+                shifted = keep.tile([P, E], F32)
+                nc.gpsimd.tensor_scalar(
+                    out=shifted[:], in0=ys[t][:], scalar1=1.0, scalar2=neg_mean[:, t : t + 1], op0=ALU.mult, op1=ALU.add
+                )
+                nc.gpsimd.tensor_tensor(out=centred[:], in0=shifted[:], in1=gamma_sb[:], op=ALU.mult)
+            else:
+                nc.vector.scalar_tensor_tensor(
+                    out=centred[:],
+                    in0=ys[t][:],
+                    scalar=neg_mean[:, t : t + 1],
+                    in1=gamma_all[:],
+                    op0=ALU.add,
+                    op1=ALU.mult,
+                )
             centred_of.append(centred)
         for t in range(TILES):
             j, b = divmod(t, B)

@@ -23,6 +23,9 @@ E_CHUNKS = E // P
 LN_EPS = 1e-6
 GPSIMD_TILE = TILES - 1
 
+WARM_COLS = 256
+WARM_PASSES = 3
+
 FLOPS = 2 * B * S * E * E
 
 
@@ -44,6 +47,12 @@ def tile_selfattention_pa_s_kernel(tc, h_attn, x, out_w_words, out_w_scales, ln_
         ident_bf = keep.tile([P, P], BF16)
         one = keep.tile([P, 1], F32)
         warm = keep.tile([P, 1], F32)
+
+        zeros = keep.tile([P, WARM_COLS], F32)
+        nc.vector.memset(zeros[:], 0.0)
+        scratch = psum_gb.tile([P, WARM_COLS], F32)
+        for i in range(WARM_PASSES):
+            nc.tensor.matmul(out=scratch[:], lhsT=zeros[:, 0:P], rhs=zeros[:], start=True, stop=True)
 
         nc.vector.memset(w_plane[:].bitcast(I32), 0)
         for j in range(S_BLOCKS):

@@ -161,10 +161,17 @@ def tile_selfattention_pa_s_kernel(tc, h_attn, x, out_w_words, out_w_scales, ln_
                 accum_out=sq_sum[:, t : t + 1],
             )
             ys.append(y)
-        nc.scalar.activation(out=rstd[:], in_=sq_sum[:], func=ACT.Abs_reciprocal_sqrt, bias=LN_EPS, scale=1.0 / E)
-
+            if t % 2 == 1:
+                nc.scalar.activation(
+                    out=rstd[:, t - 1 : t + 1],
+                    in_=sq_sum[:, t - 1 : t + 1],
+                    func=ACT.Abs_reciprocal_sqrt,
+                    bias=LN_EPS,
+                    scale=1.0 / E,
+                )
         centred_of = []
-        for t in range(TILES):
+
+        def centre(t):
             centred = work.tile([P, E], F32)
             if t == GPSIMD_TILE:
                 shifted = keep.tile([P, E], F32)
@@ -182,10 +189,26 @@ def tile_selfattention_pa_s_kernel(tc, h_attn, x, out_w_words, out_w_scales, ln_
                     op1=ALU.mult,
                 )
             centred_of.append(centred)
-        for t in range(TILES):
+
+        def finish(t):
             j, b = divmod(t, B)
             result = work.tile([P, E], F32)
-            nc.vector.scalar_tensor_tensor(
-                out=result[:], in0=centred_of[t][:], scalar=rstd[:, t : t + 1], in1=beta_all[:], op0=ALU.mult, op1=ALU.add
-            )
-            nc.sync.dma_start(out=out[b, j * P : (j + 1) * P, :], in_=result[:])
+            pieces = 2 if t == TILES - 1 else 1
+            width = E // pieces
+            for c in range(pieces):
+                cols = slice(c * width, (c + 1) * width)
+                nc.vector.scalar_tensor_tensor(
+                    out=result[:, cols],
+                    in0=centred_of[t][:, cols],
+                    scalar=rstd[:, t : t + 1],
+                    in1=beta_all[:, cols],
+                    op0=ALU.mult,
+                    op1=ALU.add,
+                )
+                nc.sync.dma_start(out=out[b, j * P : (j + 1) * P, cols], in_=result[:, cols])
+
+        centre(0)
+        for t in range(1, TILES):
+            centre(t)
+            finish(t - 1)
+        finish(TILES - 1)

@@ -21,7 +21,7 @@ TILES = B * S_BLOCKS
 WORDS = E // 2
 E_CHUNKS = E // P
 LN_EPS = 1e-6
-GPSIMD_TILE = TILES - 1
+GPSIMD_TILES = (1, 3)
 
 WARM_COLS = 256
 WARM_PASSES = 3
@@ -69,11 +69,11 @@ def tile_selfattention_pa_s_kernel(tc, h_attn, x, out_w_words, out_w_scales, ln_
                 in_=x[:, j * P : (j + 1) * P, :].rearrange("b s e -> s b e"),
             )
         gamma_sb = keep.tile([P, E], BF16)
-        nc.sync.dma_start(out=gamma_sb[:], in_=ln_gamma.partition_broadcast(P))
         make_identity(nc, ident[:])
         nc.gpsimd.memset(gb_rows[:], 0.0)
         nc.gpsimd.dma_start(out=gb_rows[0:E_CHUNKS, :], in_=ln_gamma.rearrange("(c k) -> c k", k=P))
         nc.gpsimd.dma_start(out=gb_rows[E_CHUNKS : 2 * E_CHUNKS, :], in_=ln_beta.rearrange("(c k) -> c k", k=P))
+        nc.gpsimd.dma_start(out=gamma_sb[:], in_=ln_gamma.partition_broadcast(P))
         nc.vector.memset(one[:], 1.0)
         nc.vector.tensor_copy(out=ident_bf[:], in_=ident[:])
         nc.scalar.activation(out=warm[:], in_=one[:], func=ACT.Abs_reciprocal_sqrt)
@@ -113,7 +113,8 @@ def tile_selfattention_pa_s_kernel(tc, h_attn, x, out_w_words, out_w_scales, ln_
             quantise_and_multiply(t)
 
         gb_cols = keep.tile([P, 2 * E_CHUNKS], BF16)
-        nc.scalar.copy(out=gb_cols[:], in_=gb_t[:, 0 : 2 * E_CHUNKS])
+        nc.scalar.activation(out=gb_cols[:, 0:E_CHUNKS], in_=gb_t[:, 0:E_CHUNKS], func=ACT.Copy, scale=1.0 * E)
+        nc.scalar.copy(out=gb_cols[:, E_CHUNKS : 2 * E_CHUNKS], in_=gb_t[:, E_CHUNKS : 2 * E_CHUNKS])
         gamma_all = psum_gb.tile([P, E], BF16)
         beta_all = psum_gb.tile([P, E], BF16)
         for c in range(E_CHUNKS):
@@ -132,17 +133,50 @@ def tile_selfattention_pa_s_kernel(tc, h_attn, x, out_w_words, out_w_scales, ln_
         sq_sum = keep.tile([P, TILES], F32)
         rstd = keep.tile([P, TILES], F32)
         ys = []
-        for t in range(TILES):
+        shifted_of = {}
+        centred_of = {}
+
+        def add_residual(t):
             y = work.tile([P, E], F32)
             nc.vector.scalar_tensor_tensor(
                 out=y[:],
                 in0=banks[t][:],
-                scalar=1.0,
+                scalar=-1.0 if t in GPSIMD_TILES else 1.0,
                 in1=x_sb[:, t, :],
                 op0=ALU.mult,
-                op1=ALU.add,
+                op1=ALU.subtract if t in GPSIMD_TILES else ALU.add,
                 accum_out=y_sum[:, t : t + 1],
             )
+            ys.append(y)
+
+        def shift(t):
+            shifted = work.tile([P, E], F32)
+            nc.scalar.activation(
+                out=shifted[:], in_=ys[t][:], func=ACT.Identity, bias=y_sum[:, t : t + 1], scale=-1.0 * E
+            )
+            shifted_of[t] = shifted
+
+        def sum_squares(t):
+            squares = work.tile([P, E], F32)
+            nc.scalar.activation(
+                out=squares[:],
+                in_=ys[t][:],
+                func=ACT.Square,
+                bias=y_sum[:, t : t + 1],
+                scale=-1.0 * E,
+                accum_out=sq_sum[:, t : t + 1],
+            )
+
+        def inverse_deviation(t0, t1):
+            nc.scalar.activation(
+                out=rstd[:, t0:t1],
+                in_=sq_sum[:, t0:t1],
+                func=ACT.Abs_reciprocal_sqrt,
+                bias=LN_EPS * E * E,
+                scale=1.0 / E,
+            )
+
+        def minus_mean(t):
             nc.gpsimd.tensor_scalar(
                 out=neg_mean[:, t : t + 1],
                 in0=y_sum[:, t : t + 1],
@@ -151,34 +185,11 @@ def tile_selfattention_pa_s_kernel(tc, h_attn, x, out_w_words, out_w_scales, ln_
                 op0=ALU.mult,
                 op1=ALU.add,
             )
-            squares = work.tile([P, E], F32)
-            nc.scalar.activation(
-                out=squares[:],
-                in_=y[:],
-                func=ACT.Square,
-                bias=neg_mean[:, t : t + 1],
-                scale=1.0,
-                accum_out=sq_sum[:, t : t + 1],
-            )
-            ys.append(y)
-            if t % 2 == 1:
-                nc.scalar.activation(
-                    out=rstd[:, t - 1 : t + 1],
-                    in_=sq_sum[:, t - 1 : t + 1],
-                    func=ACT.Abs_reciprocal_sqrt,
-                    bias=LN_EPS,
-                    scale=1.0 / E,
-                )
-        centred_of = []
 
         def centre(t):
             centred = work.tile([P, E], F32)
-            if t == GPSIMD_TILE:
-                shifted = keep.tile([P, E], F32)
-                nc.gpsimd.tensor_scalar(
-                    out=shifted[:], in0=ys[t][:], scalar1=1.0, scalar2=neg_mean[:, t : t + 1], op0=ALU.mult, op1=ALU.add
-                )
-                nc.gpsimd.tensor_tensor(out=centred[:], in0=shifted[:], in1=gamma_sb[:], op=ALU.mult)
+            if t in GPSIMD_TILES:
+                nc.gpsimd.tensor_tensor(out=centred[:], in0=shifted_of[t][:], in1=gamma_sb[:], op=ALU.mult)
             else:
                 nc.vector.scalar_tensor_tensor(
                     out=centred[:],
@@ -188,7 +199,7 @@ def tile_selfattention_pa_s_kernel(tc, h_attn, x, out_w_words, out_w_scales, ln_
                     op0=ALU.add,
                     op1=ALU.mult,
                 )
-            centred_of.append(centred)
+            centred_of[t] = centred
 
         def finish(t):
             j, b = divmod(t, B)
@@ -207,8 +218,24 @@ def tile_selfattention_pa_s_kernel(tc, h_attn, x, out_w_words, out_w_scales, ln_
                 )
                 nc.sync.dma_start(out=out[b, j * P : (j + 1) * P, cols], in_=result[:, cols])
 
+        add_residual(0)
+        minus_mean(0)
+        sum_squares(0)
+        add_residual(1)
+        shift(1)
+        sum_squares(1)
+        add_residual(2)
+        minus_mean(2)
+        centre(1)
+        add_residual(3)
+        shift(3)
+        inverse_deviation(0, 2)
+        sum_squares(2)
+        inverse_deviation(2, 3)
+        sum_squares(3)
+        inverse_deviation(3, 4)
+        centre(3)
         centre(0)
-        for t in range(1, TILES):
-            centre(t)
-            finish(t - 1)
-        finish(TILES - 1)
+        centre(2)
+        for t in range(TILES):
+            finish(t)

@@ -24,7 +24,7 @@ LN_EPS = 1e-6
 GPSIMD_TILES = (1, 3)
 
 WARM_COLS = 256
-WARM_PASSES = 3
+WARM_PASSES = 2
 
 FLOPS = 2 * B * S * E * E
 
@@ -69,24 +69,26 @@ def tile_selfattention_pa_s_kernel(tc, h_attn, x, out_w_words, out_w_scales, ln_
                 in_=x[:, j * P : (j + 1) * P, :].rearrange("b s e -> s b e"),
             )
         gamma_sb = keep.tile([P, E], BF16)
+        nc.sync.dma_start(out=gamma_sb[:], in_=ln_gamma.partition_broadcast(P))
         make_identity(nc, ident[:])
         nc.gpsimd.memset(gb_rows[:], 0.0)
         nc.gpsimd.dma_start(out=gb_rows[0:E_CHUNKS, :], in_=ln_gamma.rearrange("(c k) -> c k", k=P))
         nc.gpsimd.dma_start(out=gb_rows[E_CHUNKS : 2 * E_CHUNKS, :], in_=ln_beta.rearrange("(c k) -> c k", k=P))
-        nc.gpsimd.dma_start(out=gamma_sb[:], in_=ln_gamma.partition_broadcast(P))
         nc.vector.memset(one[:], 1.0)
         nc.vector.tensor_copy(out=ident_bf[:], in_=ident[:])
         nc.scalar.activation(out=warm[:], in_=one[:], func=ACT.Abs_reciprocal_sqrt)
 
         banks = []
-        for t in range(TILES):
+        codes_of = []
+
+        def transpose_tile(t):
             bank = psum.tile([P, E], F32)
             h_words = h_sb[:, t, :].bitcast(F32)
             for u in range(2):
                 nc.tensor.transpose(bank[:, u * P : (u + 1) * P], h_words[:, u:WORDS:2], ident[:])
             banks.append(bank)
 
-        def quantise_and_multiply(t):
+        def quantise(t):
             grouped = work.tile([P, 4 * P], BF16, align_bytes=64)
             nc.scalar.copy(
                 out=grouped[:].bitcast(F32).rearrange("p (r u) -> p r u", u=2),
@@ -95,6 +97,10 @@ def tile_selfattention_pa_s_kernel(tc, h_attn, x, out_w_words, out_w_scales, ln_
             m_codes = work.tile([P, P], U32, align_bytes=64)
             m_scales = work.tile([P, P], U8, align_bytes=64)
             nc.vector.quantize_mx(out=m_codes[:].bitcast(FP8X4), scales=m_scales[:], in_=grouped[:])
+            codes_of.append((m_codes, m_scales))
+
+        def multiply(t):
+            m_codes, m_scales = codes_of[t]
             nc.tensor.matmul_mx(
                 out=banks[t][:],
                 lhsT=m_codes[:].bitcast(FP8X4),
@@ -106,27 +112,9 @@ def tile_selfattention_pa_s_kernel(tc, h_attn, x, out_w_words, out_w_scales, ln_
             )
 
         gb_t = psum_gb.tile([P, P], BF16)
-        for t in range(TILES // 2):
-            quantise_and_multiply(t)
-        nc.tensor.transpose(gb_t[:], gb_rows[:], ident_bf[:])
-        for t in range(TILES // 2, TILES):
-            quantise_and_multiply(t)
-
         gb_cols = keep.tile([P, 2 * E_CHUNKS], BF16)
-        nc.scalar.activation(out=gb_cols[:, 0:E_CHUNKS], in_=gb_t[:, 0:E_CHUNKS], func=ACT.Copy, scale=1.0 * E)
-        nc.scalar.copy(out=gb_cols[:, E_CHUNKS : 2 * E_CHUNKS], in_=gb_t[:, E_CHUNKS : 2 * E_CHUNKS])
         gamma_all = psum_gb.tile([P, E], BF16)
         beta_all = psum_gb.tile([P, E], BF16)
-        for c in range(E_CHUNKS):
-            nc.tensor.transpose(
-                gamma_all[:, c * P : (c + 1) * P], gb_cols[:, c : c + 1].to_broadcast([P, P]), ident_bf[:]
-            )
-        for c in range(E_CHUNKS):
-            nc.tensor.transpose(
-                beta_all[:, c * P : (c + 1) * P],
-                gb_cols[:, E_CHUNKS + c : E_CHUNKS + c + 1].to_broadcast([P, P]),
-                ident_bf[:],
-            )
 
         y_sum = keep.tile([P, TILES], F32)
         neg_mean = keep.tile([P, TILES], F32)
@@ -218,8 +206,31 @@ def tile_selfattention_pa_s_kernel(tc, h_attn, x, out_w_words, out_w_scales, ln_
                 )
                 nc.sync.dma_start(out=out[b, j * P : (j + 1) * P, cols], in_=result[:, cols])
 
+        for t in range(TILES):
+            transpose_tile(t)
+        quantise(0)
+        multiply(0)
+        quantise(1)
+        multiply(1)
+        nc.tensor.transpose(gb_t[:], gb_rows[:], ident_bf[:])
+        quantise(2)
+        multiply(2)
         add_residual(0)
         minus_mean(0)
+        quantise(3)
+        multiply(3)
+        nc.scalar.activation(out=gb_cols[:, 0:E_CHUNKS], in_=gb_t[:, 0:E_CHUNKS], func=ACT.Copy, scale=1.0 * E)
+        nc.scalar.copy(out=gb_cols[:, E_CHUNKS : 2 * E_CHUNKS], in_=gb_t[:, E_CHUNKS : 2 * E_CHUNKS])
+        for c in range(E_CHUNKS):
+            nc.tensor.transpose(
+                gamma_all[:, c * P : (c + 1) * P], gb_cols[:, c : c + 1].to_broadcast([P, P]), ident_bf[:]
+            )
+        for c in range(E_CHUNKS):
+            nc.tensor.transpose(
+                beta_all[:, c * P : (c + 1) * P],
+                gb_cols[:, E_CHUNKS + c : E_CHUNKS + c + 1].to_broadcast([P, P]),
+                ident_bf[:],
+            )
         sum_squares(0)
         add_residual(1)
         shift(1)

from contextlib import ExitStack

import concourse.mybir as mybir
from concourse.masks import make_identity

F32 = mybir.dt.float32
BF16 = mybir.dt.bfloat16
I32 = mybir.dt.int32
U32 = mybir.dt.uint32
U8 = mybir.dt.uint8
FP8X4 = mybir.dt.float8_e4m3fn_x4
FP4X4 = mybir.dt.float4_e2m1fn_x4
ALU = mybir.AluOpType
ACT = mybir.ActivationFunctionType

P = 128
B, H, S, D = 2, 4, 256, 128
E = H * D
S_BLOCKS = S // P
TILES = B * S_BLOCKS
WORDS = E // 2
E_CHUNKS = E // P
LN_EPS = 1e-6
GPSIMD_TILES = (1, 3)

WARM_COLS = 256
WARM_PASSES = 2

FLOPS = 2 * B * S * E * E


def tile_selfattention_pa_s_kernel(tc, h_attn, x, out_w_words, out_w_scales, ln_gamma, ln_beta, out):
    nc = tc.nc
    with ExitStack() as ctx:
        ctx.enter_context(tc.manual_schedule())
        keep = ctx.enter_context(tc.tile_pool(name="keep", bufs=1))
        work = ctx.enter_context(tc.tile_pool(name="work", bufs=TILES))
        psum = ctx.enter_context(tc.psum_pool(name="psum", bufs=TILES))
        psum_gb = ctx.enter_context(tc.psum_pool(name="psum_gb", bufs=1))

        h_sb = keep.tile([P, TILES, E], BF16)
        x_sb = keep.tile([P, TILES, E], BF16)
        w_words = keep.tile([P, 2 * E], U8, align_bytes=64)
        w_plane = keep.tile([P, E], U8, align_bytes=64)
        gb_rows = keep.tile([P, P], BF16)
        ident = keep.tile([P, P], F32)
        ident_bf = keep.tile([P, P], BF16)
        one = keep.tile([P, 1], F32)
        warm = keep.tile([P, 1], F32)

        zeros = keep.tile([P, WARM_COLS], F32)
        nc.vector.memset(zeros[:], 0.0)
        scratch = psum_gb.tile([P, WARM_COLS], F32)
        for i in range(WARM_PASSES):
            nc.tensor.matmul(out=scratch[:], lhsT=zeros[:, 0:P], rhs=zeros[:], start=True, stop=True)

        nc.vector.memset(w_plane[:].bitcast(I32), 0)
        for j in range(S_BLOCKS):
            nc.sync.dma_start(
                out=h_sb[:, B * j : B * (j + 1), :].rearrange("p t (h d) -> p (t h) d", d=D),
                in_=h_attn[:, :, j * P : (j + 1) * P, :].rearrange("b h s d -> s (b h) d"),
            )
        nc.sync.dma_start(out=w_words[:].bitcast(I32), in_=out_w_words[0].bitcast(I32))
        for r in range(4):
            nc.sync.dma_start(out=w_plane[r:P:32, :].bitcast(I32), in_=out_w_scales[0, r:16:4, :].bitcast(I32))
        for j in range(S_BLOCKS):
            nc.sync.dma_start(
                out=x_sb[:, B * j : B * (j + 1), :],
                in_=x[:, j * P : (j + 1) * P, :].rearrange("b s e -> s b e"),
            )
        gamma_sb = keep.tile([P, E], BF16)
        nc.sync.dma_start(out=gamma_sb[:], in_=ln_gamma.partition_broadcast(P))
        make_identity(nc, ident[:])
        nc.gpsimd.memset(gb_rows[:], 0.0)
        nc.gpsimd.dma_start(out=gb_rows[0:E_CHUNKS, :], in_=ln_gamma.rearrange("(c k) -> c k", k=P))
        nc.gpsimd.dma_start(out=gb_rows[E_CHUNKS : 2 * E_CHUNKS, :], in_=ln_beta.rearrange("(c k) -> c k", k=P))
        nc.vector.memset(one[:], 1.0)
        nc.vector.tensor_copy(out=ident_bf[:], in_=ident[:])
        nc.scalar.activation(out=warm[:], in_=one[:], func=ACT.Abs_reciprocal_sqrt)

        banks = []
        codes_of = []

        def transpose_tile(t):
            bank = psum.tile([P, E], F32)
            h_words = h_sb[:, t, :].bitcast(F32)
            for u in range(2):
                nc.tensor.transpose(bank[:, u * P : (u + 1) * P], h_words[:, u:WORDS:2], ident[:])
            banks.append(bank)

        def quantise(t):
            grouped = work.tile([P, 4 * P], BF16, align_bytes=64)
            nc.scalar.copy(
                out=grouped[:].bitcast(F32).rearrange("p (r u) -> p r u", u=2),
                in_=banks[t][:, 0 : 2 * P].rearrange("p (u r) -> p r u", u=2),
            )
            m_codes = work.tile([P, P], U32, align_bytes=64)
            m_scales = work.tile([P, P], U8, align_bytes=64)
            nc.vector.quantize_mx(out=m_codes[:].bitcast(FP8X4), scales=m_scales[:], in_=grouped[:])
            codes_of.append((m_codes, m_scales))

        def multiply(t):
            m_codes, m_scales = codes_of[t]
            nc.tensor.matmul_mx(
                out=banks[t][:],
                lhsT=m_codes[:].bitcast(FP8X4),
                lhsT_scale=m_scales[:],
                rhs=w_words[:].bitcast(FP4X4),
                rhs_scale=w_plane[:],
                start=True,
                stop=True,
            )

        gb_t = psum_gb.tile([P, P], BF16)
        gb_cols = keep.tile([P, 2 * E_CHUNKS], BF16)
        gamma_all = psum_gb.tile([P, E], BF16)
        beta_all = psum_gb.tile([P, E], BF16)

        y_sum = keep.tile([P, TILES], F32)
        neg_mean = keep.tile([P, TILES], F32)
        sq_sum = keep.tile([P, TILES], F32)
        rstd = keep.tile([P, TILES], F32)
        ys = []
        shifted_of = {}
        centred_of = {}

        def add_residual(t):
            y = work.tile([P, E], F32)
            nc.vector.scalar_tensor_tensor(
                out=y[:],
                in0=banks[t][:],
                scalar=-1.0 if t in GPSIMD_TILES else 1.0,
                in1=x_sb[:, t, :],
                op0=ALU.mult,
                op1=ALU.subtract if t in GPSIMD_TILES else ALU.add,
                accum_out=y_sum[:, t : t + 1],
            )
            ys.append(y)

        def shift(t):
            shifted = work.tile([P, E], F32)
            nc.scalar.activation(
                out=shifted[:], in_=ys[t][:], func=ACT.Identity, bias=y_sum[:, t : t + 1], scale=-1.0 * E
            )
            shifted_of[t] = shifted

        def sum_squares(t):
            squares = work.tile([P, E], F32)
            nc.scalar.activation(
                out=squares[:],
                in_=ys[t][:],
                func=ACT.Square,
                bias=y_sum[:, t : t + 1],
                scale=-1.0 * E,
                accum_out=sq_sum[:, t : t + 1],
            )

        def inverse_deviation(t0, t1):
            nc.scalar.activation(
                out=rstd[:, t0:t1],
                in_=sq_sum[:, t0:t1],
                func=ACT.Abs_reciprocal_sqrt,
                bias=LN_EPS * E * E,
                scale=1.0 / E,
            )

        def minus_mean(t):
            nc.gpsimd.tensor_scalar(
                out=neg_mean[:, t : t + 1],
                in0=y_sum[:, t : t + 1],
                scalar1=-1.0 / E,
                scalar2=0.0,
                op0=ALU.mult,
                op1=ALU.add,
            )

        def centre(t):
            centred = work.tile([P, E], F32)
            if t in GPSIMD_TILES:
                nc.gpsimd.tensor_tensor(out=centred[:], in0=shifted_of[t][:], in1=gamma_sb[:], op=ALU.mult)
            else:
                nc.vector.scalar_tensor_tensor(
                    out=centred[:],
                    in0=ys[t][:],
                    scalar=neg_mean[:, t : t + 1],
                    in1=gamma_all[:],
                    op0=ALU.add,
                    op1=ALU.mult,
                )
            centred_of[t] = centred

        def finish(t):
            j, b = divmod(t, B)
            result = work.tile([P, E], F32)
            pieces = 2 if t == TILES - 1 else 1
            width = E // pieces
            for c in range(pieces):
                cols = slice(c * width, (c + 1) * width)
                nc.vector.scalar_tensor_tensor(
                    out=result[:, cols],
                    in0=centred_of[t][:, cols],
                    scalar=rstd[:, t : t + 1],
                    in1=beta_all[:, cols],
                    op0=ALU.mult,
                    op1=ALU.add,
                )
                nc.sync.dma_start(out=out[b, j * P : (j + 1) * P, cols], in_=result[:, cols])

        for t in range(TILES):
            transpose_tile(t)
        quantise(0)
        multiply(0)
        quantise(1)
        multiply(1)
        nc.tensor.transpose(gb_t[:], gb_rows[:], ident_bf[:])
        quantise(2)
        multiply(2)
        add_residual(0)
        minus_mean(0)
        quantise(3)
        multiply(3)
        nc.scalar.activation(out=gb_cols[:, 0:E_CHUNKS], in_=gb_t[:, 0:E_CHUNKS], func=ACT.Copy, scale=1.0 * E)
        nc.scalar.copy(out=gb_cols[:, E_CHUNKS : 2 * E_CHUNKS], in_=gb_t[:, E_CHUNKS : 2 * E_CHUNKS])
        for c in range(E_CHUNKS):
            nc.tensor.transpose(
                gamma_all[:, c * P : (c + 1) * P], gb_cols[:, c : c + 1].to_broadcast([P, P]), ident_bf[:]
            )
        for c in range(E_CHUNKS):
            nc.tensor.transpose(
                beta_all[:, c * P : (c + 1) * P],
                gb_cols[:, E_CHUNKS + c : E_CHUNKS + c + 1].to_broadcast([P, P]),
                ident_bf[:],
            )
        sum_squares(0)
        add_residual(1)
        shift(1)
        sum_squares(1)
        add_residual(2)
        minus_mean(2)
        centre(1)
        add_residual(3)
        shift(3)
        inverse_deviation(0, 2)
        sum_squares(2)
        inverse_deviation(2, 3)
        sum_squares(3)
        inverse_deviation(3, 4)
        centre(3)
        centre(0)
        centre(2)
        for t in range(TILES):
            finish(t)
